import numpy as np
import ml_dtypes


def mxq(x, axis, fmt="e4m3"):
    dtype, down = {"e4m3": (ml_dtypes.float8_e4m3fn, 7), "e5m2": (ml_dtypes.float8_e5m2, 14)}[fmt]
    v = np.moveaxis(np.asarray(x, np.float32).astype(ml_dtypes.bfloat16).astype(np.float64), axis, -1)
    blocks = v.reshape(v.shape[:-1] + (-1, 32))
    amax = np.abs(blocks).max(-1, keepdims=True)
    byte = np.maximum(np.where(amax > 0, np.frexp(amax)[1] - 1 + 127, 0) - down, 1)
    scale = np.exp2(byte - 127.0)
    codes = (blocks / scale).astype(np.float32).astype(dtype).astype(np.float64)
    return np.moveaxis((codes * scale).reshape(v.shape), -1, axis)


WIDE = False


def mx_kscale(k):
    if not WIDE:
        return np.ones(k)
    levels = np.array([20, -20, 10, -10, 0])
    a = np.random.permutation(np.resize(levels, k // 512 * 4)).reshape(k // 512, 4)
    idx = np.arange(k)
    return np.exp2(a[idx // 512, idx % 128 // 32])


BF16 = ml_dtypes.bfloat16


def bf(x):
    return np.asarray(x, np.float32).astype(BF16)


def f64(x):
    return np.asarray(x).astype(np.float64)


B, P, D, H = 4, 2048, 512, 512

QMAX = 127
STEP = 2.0 ** np.round(np.log2(4.0 / np.sqrt(D) / QMAX))


def setup_inputs():
    u = mx_kscale(H)
    w = np.clip(np.round(np.random.standard_normal((H, D)) / np.sqrt(D) / STEP), -QMAX, QMAX) * STEP
    w.flat[np.random.randint(w.size)] = -QMAX * STEP
    w = w / u[:, None]
    pv = np.random.randint(0, 3, (B, P, D)) * 0.5
    pe = np.random.standard_normal((P, H)) * 0.5
    g = np.random.standard_normal((B, P, H)) * np.exp2(np.random.randint(-12, 1, (B, P, 1))) * 8.0 * u
    return {"pixel_values": bf(pv), "proj_weight": bf(w), "pos_emb": bf(pe), "grad_out": bf(g)}


def reference(pixel_values, proj_weight, pos_emb, grad_out):
    g = mxq(f64(grad_out), 2, "e5m2")
    w = mxq(f64(proj_weight), 0, "e4m3")
    return 2.0 * (g @ w)

@@ -1,0 +1,133 @@
+from contextlib import ExitStack
+
+import concourse.mybir as mybir
+from concourse.masks import make_identity
+
+F32 = mybir.dt.float32
+BF16 = mybir.dt.bfloat16
+U32 = mybir.dt.uint32
+U8 = mybir.dt.uint8
+E5M2X4 = mybir.dt.float8_e5m2_x4
+E4M3X4 = mybir.dt.float8_e4m3fn_x4
+
+P = 128
+TOKENS = 4 * 2048
+H = 512
+D = 512
+N_TILES = TOKENS // P
+ROUND = 4
+CHUNKS = [8, 8, 8, 8, 8, 8, 8, 8]
+
+FLOPS = 2 * TOKENS * H * D
+BYTES = TOKENS * H * 2 + H * D * 2 + TOKENS * D * 4
+
+
+def tile_patchembedding_t_kernel(tc, pixel_values, proj_weight, pos_emb, grad_out, out):
+    nc = tc.nc
+    g_rows = grad_out.flatten_outer_dims()
+    out_rows = out.flatten_outer_dims()
+    assert sum(CHUNKS) == N_TILES
+
+    with ExitStack() as ctx:
+        keep = ctx.enter_context(tc.tile_pool(name="keep", bufs=1))
+        work = ctx.enter_context(tc.tile_pool(name="work", bufs=3))
+        tp_pool = ctx.enter_context(tc.psum_pool(name="tp", bufs=4))
+        acc_pool = ctx.enter_context(tc.psum_pool(name="acc", bufs=4))
+        ctx.enter_context(tc.manual_schedule())
+
+        w_raw = keep.tile([P, 4, D], BF16, name="w_raw")
+        nc.sync.dma_start(
+            out=w_raw[:].rearrange("p (u e) c -> p u e c", u=2),
+            in_=proj_weight.rearrange("(u q e) c -> q u e c", u=2, e=2),
+        )
+        g_of = []
+        stage_of = []
+        store_after = {}
+        base = 0
+        for c, n in enumerate(CHUNKS):
+            g_c = keep.tile([P, n, H], BF16, name="g%d" % c)
+            nc.sync.dma_start(
+                out=g_c[:],
+                in_=g_rows[base : base + P * n, :].rearrange("(p t) h -> p t h", t=n),
+            )
+            s_c = keep.tile([P, n, D], F32, name="s%d" % c)
+            for t in range(n):
+                g_of.append(g_c[:, t, :])
+                stage_of.append(s_c[:, t, :])
+            store_after[len(g_of) - 1] = (
+                out_rows[base : base + P * n, :].rearrange("(p t) d -> p t d", t=n),
+                s_c,
+            )
+            base += P * n
+
+        ident = keep.tile([P, P], F32, name="ident")
+        make_identity(nc, ident[:])
+
+        w_grouped = keep.tile([P, D, 4], BF16, name="w_grouped", align_bytes=64)
+        nc.vector.tensor_copy(out=w_grouped[:], in_=w_raw[:].rearrange("p t c -> p c t"))
+        w_codes = keep.tile([P, D], U32, name="w_codes", align_bytes=64)
+        w_scales = keep.tile([P, D], U8, name="w_scales", align_bytes=64)
+        nc.vector.quantize_mx(
+            out=w_codes[:].bitcast(E4M3X4),
+            scales=w_scales[:],
+            in_=w_grouped[:].rearrange("p c t -> p (c t)"),
+        )
+
+        grouped_of = {}
+        codes_of = {}
+
+        def transposes(r):
+            grouped = work.tile([P, ROUND * P * 4], BF16, name="grouped", align_bytes=64)
+            grouped_of[r] = grouped
+            words = grouped[:].bitcast(F32)
+            for half in range(ROUND // 2):
+                bank = tp_pool.tile([P, 512], F32, name="bank")
+                for j in range(2):
+                    src = g_of[ROUND * r + 2 * half + j].bitcast(F32)
+                    for u in range(2):
+                        col = (2 * j + u) * P
+                        nc.tensor.transpose(
+                            bank[:, col : col + P], src[:, u * P : (u + 1) * P], ident[:]
+                        )
+                nc.vector.tensor_copy(
+                    out=words[:, 512 * half : 512 * half + 512].rearrange(
+                        "p (j r u) -> p j r u", j=2, u=2
+                    ),
+                    in_=bank[:].rearrange("p (j u r) -> p j r u", j=2, u=2),
+                )
+
+        def quantise(r):
+            codes = work.tile([P, ROUND * P], U32, name="codes", align_bytes=64)
+            scales = work.tile([P, ROUND * P], U8, name="scales", align_bytes=64)
+            codes_of[r] = (codes, scales)
+            nc.vector.quantize_mx(
+                out=codes[:].bitcast(E5M2X4), scales=scales[:], in_=grouped_of[r][:]
+            )
+
+        def multiply(r):
+            codes, scales = codes_of[r]
+            for j in range(ROUND):
+                i = ROUND * r + j
+                acc = acc_pool.tile([P, D], F32, name="acc")
+                nc.tensor.matmul_mx(
+                    out=acc[:],
+                    lhsT=codes[:, j * P : (j + 1) * P].bitcast(E5M2X4),
+                    lhsT_scale=scales[:, j * P : (j + 1) * P],
+                    rhs=w_codes[:].bitcast(E4M3X4),
+                    rhs_scale=w_scales[:],
+                    start=True,
+                    stop=True,
+                )
+                nc.scalar.mul(out=stage_of[i], in_=acc[:], mul=2.0)
+                if i in store_after:
+                    dst, s_c = store_after[i]
+                    nc.sync.dma_start(out=dst, in_=s_c[:])
+
+        n_rounds = N_TILES // ROUND
+        transposes(0)
+        transposes(1)
+        for r in range(n_rounds):
+            quantise(r)
+            if r + 2 < n_rounds:
+                transposes(r + 2)
+            multiply(r)

@@ -16,7 +16,8 @@ H = 512
 D = 512
 N_TILES = TOKENS // P
 ROUND = 4
-CHUNKS = [8, 8, 8, 8, 8, 8, 8, 8]
+LOADS = [8, 24, 32]
+STORES = [16, 16, 16, 16]
 
 FLOPS = 2 * TOKENS * H * D
 BYTES = TOKENS * H * 2 + H * D * 2 + TOKENS * D * 4
@@ -24,9 +25,9 @@ BYTES = TOKENS * H * 2 + H * D * 2 + TOKENS * D * 4
 
 def tile_patchembedding_t_kernel(tc, pixel_values, proj_weight, pos_emb, grad_out, out):
     nc = tc.nc
-    g_rows = grad_out.flatten_outer_dims()
-    out_rows = out.flatten_outer_dims()
-    assert sum(CHUNKS) == N_TILES
+    g_view = grad_out.flatten_outer_dims().rearrange("(p t) h -> p t h", t=N_TILES)
+    out_view = out.flatten_outer_dims().rearrange("(p t) d -> p t d", t=N_TILES)
+    assert sum(LOADS) == N_TILES and sum(STORES) == N_TILES
 
     with ExitStack() as ctx:
         keep = ctx.enter_context(tc.tile_pool(name="keep", bufs=1))
@@ -43,22 +44,18 @@ def tile_patchembedding_t_kernel(tc, pixel_values, proj_weight, pos_emb, grad_ou
         g_of = []
         stage_of = []
         store_after = {}
-        base = 0
-        for c, n in enumerate(CHUNKS):
+        for c, n in enumerate(LOADS):
             g_c = keep.tile([P, n, H], BF16, name="g%d" % c)
-            nc.sync.dma_start(
-                out=g_c[:],
-                in_=g_rows[base : base + P * n, :].rearrange("(p t) h -> p t h", t=n),
-            )
-            s_c = keep.tile([P, n, D], F32, name="s%d" % c)
+            t0 = len(g_of)
+            nc.sync.dma_start(out=g_c[:], in_=g_view[:, t0 : t0 + n, :])
             for t in range(n):
                 g_of.append(g_c[:, t, :])
+        for c, n in enumerate(STORES):
+            s_c = keep.tile([P, n, D], F32, name="s%d" % c)
+            t0 = len(stage_of)
+            for t in range(n):
                 stage_of.append(s_c[:, t, :])
-            store_after[len(g_of) - 1] = (
-                out_rows[base : base + P * n, :].rearrange("(p t) d -> p t d", t=n),
-                s_c,
-            )
-            base += P * n
+            store_after[t0 + n - 1] = (out_view[:, t0 : t0 + n, :], s_c)
 
         ident = keep.tile([P, P], F32, name="ident")
         make_identity(nc, ident[:])
@@ -118,7 +115,10 @@ def tile_patchembedding_t_kernel(tc, pixel_values, proj_weight, pos_emb, grad_ou
                     start=True,
                     stop=True,
                 )
-                nc.scalar.mul(out=stage_of[i], in_=acc[:], mul=2.0)
+                if j == ROUND - 1 and r % 2 == 1:
+                    nc.vector.tensor_scalar_mul(out=stage_of[i], in0=acc[:], scalar1=2.0)
+                else:
+                    nc.scalar.mul(out=stage_of[i], in_=acc[:], mul=2.0)
                 if i in store_after:
                     dst, s_c = store_after[i]
                     nc.sync.dma_start(out=dst, in_=s_c[:])

@@ -16,8 +16,9 @@ H = 512
 D = 512
 N_TILES = TOKENS // P
 ROUND = 4
-LOADS = [8, 24, 32]
-STORES = [16, 16, 16, 16]
+LOADS = [8, 8, 8, 8, 16, 16]
+STORES = [16, 16, 16, 8, 8]
+AHEAD = 3
 
 FLOPS = 2 * TOKENS * H * D
 BYTES = TOKENS * H * 2 + H * D * 2 + TOKENS * D * 4
@@ -32,6 +33,7 @@ def tile_patchembedding_t_kernel(tc, pixel_values, proj_weight, pos_emb, grad_ou
     with ExitStack() as ctx:
         keep = ctx.enter_context(tc.tile_pool(name="keep", bufs=1))
         work = ctx.enter_context(tc.tile_pool(name="work", bufs=3))
+        packed = ctx.enter_context(tc.tile_pool(name="packed", bufs=AHEAD + 1))
         tp_pool = ctx.enter_context(tc.psum_pool(name="tp", bufs=4))
         acc_pool = ctx.enter_context(tc.psum_pool(name="acc", bufs=4))
         ctx.enter_context(tc.manual_schedule())
@@ -94,8 +96,8 @@ def tile_patchembedding_t_kernel(tc, pixel_values, proj_weight, pos_emb, grad_ou
                 )
 
         def quantise(r):
-            codes = work.tile([P, ROUND * P], U32, name="codes", align_bytes=64)
-            scales = work.tile([P, ROUND * P], U8, name="scales", align_bytes=64)
+            codes = packed.tile([P, ROUND * P], U32, name="codes", align_bytes=64)
+            scales = packed.tile([P, ROUND * P], U8, name="scales", align_bytes=64)
             codes_of[r] = (codes, scales)
             nc.vector.quantize_mx(
                 out=codes[:].bitcast(E5M2X4), scales=scales[:], in_=grouped_of[r][:]
@@ -125,9 +127,12 @@ def tile_patchembedding_t_kernel(tc, pixel_values, proj_weight, pos_emb, grad_ou
 
         n_rounds = N_TILES // ROUND
         transposes(0)
-        transposes(1)
+        for k in range(1, AHEAD):
+            transposes(k)
+            quantise(k - 1)
         for r in range(n_rounds):
-            quantise(r)
-            if r + 2 < n_rounds:
-                transposes(r + 2)
+            if r + AHEAD < n_rounds:
+                transposes(r + AHEAD)
+            if r + AHEAD - 1 < n_rounds:
+                quantise(r + AHEAD - 1)
             multiply(r)

@@ -39,7 +39,7 @@ def tile_patchembedding_t_kernel(tc, pixel_values, proj_weight, pos_emb, grad_ou
         ctx.enter_context(tc.manual_schedule())
 
         w_raw = keep.tile([P, 4, D], BF16, name="w_raw")
-        nc.sync.dma_start(
+        nc.scalar.dma_start(
             out=w_raw[:].rearrange("p (u e) c -> p u e c", u=2),
             in_=proj_weight.rearrange("(u q e) c -> q u e c", u=2, e=2),
         )
@@ -49,7 +49,7 @@ def tile_patchembedding_t_kernel(tc, pixel_values, proj_weight, pos_emb, grad_ou
         for c, n in enumerate(LOADS):
             g_c = keep.tile([P, n, H], BF16, name="g%d" % c)
             t0 = len(g_of)
-            nc.sync.dma_start(out=g_c[:], in_=g_view[:, t0 : t0 + n, :])
+            nc.scalar.dma_start(out=g_c[:], in_=g_view[:, t0 : t0 + n, :])
             for t in range(n):
                 g_of.append(g_c[:, t, :])
         for c, n in enumerate(STORES):

@@ -16,9 +16,9 @@ H = 512
 D = 512
 N_TILES = TOKENS // P
 ROUND = 4
-LOADS = [8, 8, 8, 8, 16, 16]
-STORES = [16, 16, 16, 8, 8]
-AHEAD = 3
+LOADS = [16, 16, 32]
+STORES = [8, 8, 8, 8, 8, 8, 8, 8]
+AHEAD = 2
 
 FLOPS = 2 * TOKENS * H * D
 BYTES = TOKENS * H * 2 + H * D * 2 + TOKENS * D * 4
@@ -74,6 +74,7 @@ def tile_patchembedding_t_kernel(tc, pixel_values, proj_weight, pos_emb, grad_ou
 
         grouped_of = {}
         codes_of = {}
+        n_rounds = N_TILES // ROUND
 
         def transposes(r):
             grouped = work.tile([P, ROUND * P * 4], BF16, name="grouped", align_bytes=64)
@@ -88,7 +89,8 @@ def tile_patchembedding_t_kernel(tc, pixel_values, proj_weight, pos_emb, grad_ou
                         nc.tensor.transpose(
                             bank[:, col : col + P], src[:, u * P : (u + 1) * P], ident[:]
                         )
-                nc.vector.tensor_copy(
+                copy_out = nc.scalar.copy if (half == 1 and r <= AHEAD) else nc.vector.tensor_copy
+                copy_out(
                     out=words[:, 512 * half : 512 * half + 512].rearrange(
                         "p (j r u) -> p j r u", j=2, u=2
                     ),
@@ -117,7 +119,7 @@ def tile_patchembedding_t_kernel(tc, pixel_values, proj_weight, pos_emb, grad_ou
                     start=True,
                     stop=True,
                 )
-                if j == ROUND - 1 and r % 2 == 1:
+                if (j == ROUND - 1 and r % 2 == 1) or (j % 2 == 1 and r + AHEAD >= n_rounds):
                     nc.vector.tensor_scalar_mul(out=stage_of[i], in0=acc[:], scalar1=2.0)
                 else:
                     nc.scalar.mul(out=stage_of[i], in_=acc[:], mul=2.0)
@@ -125,7 +127,6 @@ def tile_patchembedding_t_kernel(tc, pixel_values, proj_weight, pos_emb, grad_ou
                     dst, s_c = store_after[i]
                     nc.sync.dma_start(out=dst, in_=s_c[:])
 
-        n_rounds = N_TILES // ROUND
         transposes(0)
         for k in range(1, AHEAD):
             transposes(k)

@@ -39,10 +39,11 @@ def tile_patchembedding_t_kernel(tc, pixel_values, proj_weight, pos_emb, grad_ou
         ctx.enter_context(tc.manual_schedule())
 
         w_raw = keep.tile([P, 4, D], BF16, name="w_raw")
-        nc.scalar.dma_start(
-            out=w_raw[:].rearrange("p (u e) c -> p u e c", u=2),
-            in_=proj_weight.rearrange("(u q e) c -> q u e c", u=2, e=2),
-        )
+        for u in range(2):
+            nc.scalar.dma_start(
+                out=w_raw[:, 2 * u : 2 * u + 2, :],
+                in_=proj_weight[256 * u : 256 * u + 256, :].rearrange("(q e) c -> q e c", e=2),
+            )
         g_of = []
         stage_of = []
         store_after = {}

from contextlib import ExitStack

import concourse.mybir as mybir
from concourse.masks import make_identity

F32 = mybir.dt.float32
BF16 = mybir.dt.bfloat16
U32 = mybir.dt.uint32
U8 = mybir.dt.uint8
E5M2X4 = mybir.dt.float8_e5m2_x4
E4M3X4 = mybir.dt.float8_e4m3fn_x4

P = 128
TOKENS = 4 * 2048
H = 512
D = 512
N_TILES = TOKENS // P
ROUND = 4
LOADS = [16, 16, 32]
STORES = [8, 8, 8, 8, 8, 8, 8, 8]
AHEAD = 2

FLOPS = 2 * TOKENS * H * D
BYTES = TOKENS * H * 2 + H * D * 2 + TOKENS * D * 4


def tile_patchembedding_t_kernel(tc, pixel_values, proj_weight, pos_emb, grad_out, out):
    nc = tc.nc
    g_view = grad_out.flatten_outer_dims().rearrange("(p t) h -> p t h", t=N_TILES)
    out_view = out.flatten_outer_dims().rearrange("(p t) d -> p t d", t=N_TILES)
    assert sum(LOADS) == N_TILES and sum(STORES) == N_TILES

    with ExitStack() as ctx:
        keep = ctx.enter_context(tc.tile_pool(name="keep", bufs=1))
        work = ctx.enter_context(tc.tile_pool(name="work", bufs=3))
        packed = ctx.enter_context(tc.tile_pool(name="packed", bufs=AHEAD + 1))
        tp_pool = ctx.enter_context(tc.psum_pool(name="tp", bufs=4))
        acc_pool = ctx.enter_context(tc.psum_pool(name="acc", bufs=4))
        ctx.enter_context(tc.manual_schedule())

        w_raw = keep.tile([P, 4, D], BF16, name="w_raw")
        for u in range(2):
            nc.scalar.dma_start(
                out=w_raw[:, 2 * u : 2 * u + 2, :],
                in_=proj_weight[256 * u : 256 * u + 256, :].rearrange("(q e) c -> q e c", e=2),
            )
        g_of = []
        stage_of = []
        store_after = {}
        for c, n in enumerate(LOADS):
            g_c = keep.tile([P, n, H], BF16, name="g%d" % c)
            t0 = len(g_of)
            nc.scalar.dma_start(out=g_c[:], in_=g_view[:, t0 : t0 + n, :])
            for t in range(n):
                g_of.append(g_c[:, t, :])
        for c, n in enumerate(STORES):
            s_c = keep.tile([P, n, D], F32, name="s%d" % c)
            t0 = len(stage_of)
            for t in range(n):
                stage_of.append(s_c[:, t, :])
            store_after[t0 + n - 1] = (out_view[:, t0 : t0 + n, :], s_c)

        ident = keep.tile([P, P], F32, name="ident")
        make_identity(nc, ident[:])

        w_grouped = keep.tile([P, D, 4], BF16, name="w_grouped", align_bytes=64)
        nc.vector.tensor_copy(out=w_grouped[:], in_=w_raw[:].rearrange("p t c -> p c t"))
        w_codes = keep.tile([P, D], U32, name="w_codes", align_bytes=64)
        w_scales = keep.tile([P, D], U8, name="w_scales", align_bytes=64)
        nc.vector.quantize_mx(
            out=w_codes[:].bitcast(E4M3X4),
            scales=w_scales[:],
            in_=w_grouped[:].rearrange("p c t -> p (c t)"),
        )

        grouped_of = {}
        codes_of = {}
        n_rounds = N_TILES // ROUND

        def transposes(r):
            grouped = work.tile([P, ROUND * P * 4], BF16, name="grouped", align_bytes=64)
            grouped_of[r] = grouped
            words = grouped[:].bitcast(F32)
            for half in range(ROUND // 2):
                bank = tp_pool.tile([P, 512], F32, name="bank")
                for j in range(2):
                    src = g_of[ROUND * r + 2 * half + j].bitcast(F32)
                    for u in range(2):
                        col = (2 * j + u) * P
                        nc.tensor.transpose(
                            bank[:, col : col + P], src[:, u * P : (u + 1) * P], ident[:]
                        )
                copy_out = nc.scalar.copy if (half == 1 and r <= AHEAD) else nc.vector.tensor_copy
                copy_out(
                    out=words[:, 512 * half : 512 * half + 512].rearrange(
                        "p (j r u) -> p j r u", j=2, u=2
                    ),
                    in_=bank[:].rearrange("p (j u r) -> p j r u", j=2, u=2),
                )

        def quantise(r):
            codes = packed.tile([P, ROUND * P], U32, name="codes", align_bytes=64)
            scales = packed.tile([P, ROUND * P], U8, name="scales", align_bytes=64)
            codes_of[r] = (codes, scales)
            nc.vector.quantize_mx(
                out=codes[:].bitcast(E5M2X4), scales=scales[:], in_=grouped_of[r][:]
            )

        def multiply(r):
            codes, scales = codes_of[r]
            for j in range(ROUND):
                i = ROUND * r + j
                acc = acc_pool.tile([P, D], F32, name="acc")
                nc.tensor.matmul_mx(
                    out=acc[:],
                    lhsT=codes[:, j * P : (j + 1) * P].bitcast(E5M2X4),
                    lhsT_scale=scales[:, j * P : (j + 1) * P],
                    rhs=w_codes[:].bitcast(E4M3X4),
                    rhs_scale=w_scales[:],
                    start=True,
                    stop=True,
                )
                if (j == ROUND - 1 and r % 2 == 1) or (j % 2 == 1 and r + AHEAD >= n_rounds):
                    nc.vector.tensor_scalar_mul(out=stage_of[i], in0=acc[:], scalar1=2.0)
                else:
                    nc.scalar.mul(out=stage_of[i], in_=acc[:], mul=2.0)
                if i in store_after:
                    dst, s_c = store_after[i]
                    nc.sync.dma_start(out=dst, in_=s_c[:])

        transposes(0)
        for k in range(1, AHEAD):
            transposes(k)
            quantise(k - 1)
        for r in range(n_rounds):
            if r + AHEAD < n_rounds:
                transposes(r + AHEAD)
            if r + AHEAD - 1 < n_rounds:
                quantise(r + AHEAD - 1)
            multiply(r)
